import numpy as np
import ml_dtypes


def mxq(x, axis, fmt="e4m3"):
    dtype, down = {"e4m3": (ml_dtypes.float8_e4m3fn, 7), "e5m2": (ml_dtypes.float8_e5m2, 14)}[fmt]
    v = np.moveaxis(np.asarray(x, np.float32).astype(ml_dtypes.bfloat16).astype(np.float64), axis, -1)
    blocks = v.reshape(v.shape[:-1] + (-1, 32))
    amax = np.abs(blocks).max(-1, keepdims=True)
    byte = np.maximum(np.where(amax > 0, np.frexp(amax)[1] - 1 + 127, 0) - down, 1)
    scale = np.exp2(byte - 127.0)
    codes = (blocks / scale).astype(np.float32).astype(dtype).astype(np.float64)
    return np.moveaxis((codes * scale).reshape(v.shape), -1, axis)


WIDE = False


def mx_kscale(k):
    if not WIDE:
        return np.ones(k)
    levels = np.array([10, -10, 5, -5, 0])
    a = np.random.permutation(np.resize(levels, k // 512 * 4)).reshape(k // 512, 4)
    idx = np.arange(k)
    return np.exp2(a[idx // 512, idx % 128 // 32])


BF16 = ml_dtypes.bfloat16


def bf(x):
    return np.asarray(x, np.float32).astype(BF16)


def f64(x):
    return np.asarray(x).astype(np.float64)


B, A, G, H1, H2 = 8192, 128, 5, 1024, 512
SLOPE = 0.4


def leaky(v):
    return np.where(v >= 0.0, v, SLOPE * v)


def setup_inputs():
    s, t = mx_kscale(H1), mx_kscale(H2)
    keep = np.where(np.random.uniform(size=(B, A)) > 0.2, 1.0, 0.0)
    return {"x": bf(np.random.standard_normal((B, A * G)) * np.repeat(keep, G, axis=1)),
            "h1": bf(leaky(np.random.standard_normal((B, H1))) * s),
            "W2": bf(np.random.standard_normal((H1, H2)) * 1.3 / np.sqrt(H1) / s[:, None] * t),
            "b2": bf(np.random.standard_normal(H2) * 0.3 * t),
            "W3": bf(np.random.standard_normal((H2, A)) * 2.5 / np.sqrt(H2) / t[:, None]),
            "b3": bf(np.random.standard_normal(A) * 0.5)}


def reference(x, h1, W2, b2, W3, b3):
    gsum = f64(x).reshape(B, A, G).sum(axis=-1)
    mask = gsum != 0.0
    h2 = leaky((mxq(f64(h1), 1, "e4m3") @ mxq(f64(W2), 0, "e4m3")) + f64(b2))
    logits = (mxq(h2, 1, "e4m3") @ mxq(f64(W3), 0, "e4m3")) + f64(b3)
    logits = np.where(mask, logits, -np.inf)
    e = np.exp(logits - logits.max(axis=1, keepdims=True))
    return e / e.sum(axis=1, keepdims=True)

@@ -1,0 +1,167 @@
+from contextlib import ExitStack
+
+import concourse.bass as bass
+import concourse.mybir as mybir
+import concourse.tile as tile
+from concourse.masks import make_identity
+
+F32 = mybir.dt.float32
+BF16 = mybir.dt.bfloat16
+U32 = mybir.dt.uint32
+U8 = mybir.dt.uint8
+FP8X4 = mybir.dt.float8_e4m3fn_x4
+ALU = mybir.AluOpType
+ACT = mybir.ActivationFunctionType
+AX = mybir.AxisListType
+
+P = 128
+B, A, G, H1, H2 = 8192, 128, 5, 1024, 512
+SLOPE = 0.4
+BIG = 1.0e30
+J = 4
+ROWS = P * J
+NGROUPS = B // ROWS
+FLOPS = 2 * B * (H1 * H2 + H2 * A)
+
+
+def tile_dqn_pa_t_kernel(tc, x, h1, W2, b2, W3, b3, out):
+    nc = tc.nc
+    with ExitStack() as ctx:
+        const = ctx.enter_context(tc.tile_pool(name="const", bufs=1))
+        ld = ctx.enter_context(tc.tile_pool(name="ld", bufs=4))
+        wk = ctx.enter_context(tc.tile_pool(name="wk", bufs=2))
+        ps_t = ctx.enter_context(tc.psum_pool(name="ps_t", bufs=2))
+        ps_a = ctx.enter_context(tc.psum_pool(name="ps_a", bufs=4))
+        ps_l = ctx.enter_context(tc.psum_pool(name="ps_l", bufs=1))
+
+        h1v = h1.rearrange("(g p j) k -> g p j k", p=P, j=J)
+        xv = x.rearrange("(g p j) c -> g p j c", p=P, j=J)
+        outv = out.rearrange("(g p j) a -> g p j a", p=P, j=J)
+
+        w2raw = const.tile([P, 4, 2 * H2], BF16)
+        nc.sync.dma_start(out=w2raw[:], in_=W2.rearrange("(c q e) n -> q c (e n)", c=4, e=2))
+        w3raw = const.tile([P, 4, A], BF16)
+        nc.scalar.dma_start(out=w3raw[:], in_=W3.rearrange("(p j) a -> p j a", j=4))
+        b2bf = const.tile([P, 4], BF16)
+        nc.scalar.dma_start(out=b2bf[:], in_=b2.rearrange("(p t) -> p t", t=4))
+        b3bf = const.tile([P, A], BF16)
+        nc.scalar.dma_start(out=b3bf[:], in_=b3.partition_broadcast(P))
+
+        ident = const.tile([P, P], F32)
+        make_identity(nc, ident[:])
+        identb = const.tile([P, P], BF16)
+        make_identity(nc, identb[:])
+
+        w2grp = const.tile([P, 2, 4 * H2], BF16, align_bytes=64)
+        w2c = const.tile([P, 2, H2], U32, align_bytes=64)
+        w2s = const.tile([P, 2, H2], U8, align_bytes=64)
+        for s in range(2):
+            nc.vector.tensor_copy(
+                out=w2grp[:, s, :].rearrange("q (t m j) -> q t m j", t=4, j=4),
+                in_=w2raw[:, 2 * s : 2 * s + 2, :].rearrange("q u (e m t) -> q t m (u e)", e=2, t=4),
+            )
+        for s in range(2):
+            nc.vector.quantize_mx(out=w2c[:, s, :].bitcast(FP8X4), scales=w2s[:, s, :], in_=w2grp[:, s, :])
+        w3grp = const.tile([P, A, 4], BF16, align_bytes=64)
+        w3c = const.tile([P, A], U32, align_bytes=64)
+        w3s = const.tile([P, A], U8, align_bytes=64)
+        nc.vector.tensor_copy(out=w3grp[:], in_=w3raw[:].rearrange("p j a -> p a j"))
+        b2t = const.tile([P, 4], F32)
+        nc.vector.tensor_copy(out=b2t[:], in_=b2bf[:])
+        b3bc = const.tile([P, A], F32)
+        nc.vector.tensor_copy(out=b3bc[:], in_=b3bf[:])
+        nc.vector.quantize_mx(out=w3c[:].bitcast(FP8X4), scales=w3s[:], in_=w3grp[:].rearrange("p a j -> p (a j)"))
+
+        for g in range(NGROUPS):
+            h1_sb = ld.tile([P, J, H1], BF16, tag="h1")
+            nc.sync.dma_start(out=h1_sb[:], in_=h1v[g])
+            x_sb = ld.tile([P, J, A * G], BF16, tag="x")
+            nc.sync.dma_start(out=x_sb[:], in_=xv[g])
+
+            xg = x_sb[:].rearrange("p j (a e) -> p (j a) e", e=G)
+            t34 = wk.tile([P, ROWS], F32, tag="t34")
+            fz = wk.tile([P, J, A], F32, tag="fz")
+            q = wk.tile([P, J, A], F32, tag="q")
+            nc.gpsimd.tensor_tensor(out=t34[:], in0=xg[:, :, 3], in1=xg[:, :, 4], op=ALU.add)
+            gs = ps_l.tile([P, ROWS], F32, tag="gs")
+            for e in range(3):
+                nc.tensor.matmul(out=gs[:], lhsT=identb[:], rhs=xg[:, :, e], start=(e == 0), stop=(e == 2))
+            nc.vector.scalar_tensor_tensor(
+                out=fz[:].rearrange("p j a -> p (j a)"), in0=gs[:], scalar=-1.0, in1=t34[:],
+                op0=ALU.mult, op1=ALU.is_equal,
+            )
+            nc.vector.scalar_tensor_tensor(
+                out=q[:], in0=fz[:], scalar=-BIG, in1=b3bc[:].unsqueeze(1).to_broadcast([P, J, A]),
+                op0=ALU.mult, op1=ALU.add,
+            )
+
+            grp = wk.tile([P, 2, 4 * ROWS], BF16, align_bytes=64, tag="grp")
+            c1 = wk.tile([P, 2, ROWS], U32, align_bytes=64, tag="c1")
+            s1 = wk.tile([P, 2, ROWS], U8, align_bytes=64, tag="s1")
+            for s in range(2):
+                for jp in range(2):
+                    xt = ps_t.tile([P, 2, 2, P], F32, tag="xt")
+                    for jj in range(2):
+                        for u in range(2):
+                            c = 2 * s + u
+                            nc.tensor.transpose(
+                                xt[:, jj, u, :],
+                                h1_sb[:, 2 * jp + jj, :].bitcast(F32)[:, P * c : P * (c + 1)],
+                                ident[:],
+                            )
+                    dst = grp[:, s, :].bitcast(F32).rearrange("p (j r u) -> p j r u", j=J, u=2)
+                    nc.scalar.copy(out=dst[:, 2 * jp : 2 * jp + 2], in_=xt[:].rearrange("p j u r -> p j r u"))
+                nc.vector.quantize_mx(out=c1[:, s, :].bitcast(FP8X4), scales=s1[:, s, :], in_=grp[:, s, :])
+
+            v = wk.tile([P, 4, ROWS], F32, tag="v")
+            for t in range(4):
+                acc = ps_a.tile([P, ROWS], F32, tag="acc")
+                for s in range(2):
+                    nc.tensor.matmul_mx(
+                        out=acc[:],
+                        lhsT=w2c[:, s, P * t : P * (t + 1)].bitcast(FP8X4),
+                        lhsT_scale=w2s[:, s, P * t : P * (t + 1)],
+                        rhs=c1[:, s, :].bitcast(FP8X4),
+                        rhs_scale=s1[:, s, :],
+                        start=(s == 0),
+                        stop=(s == 1),
+                    )
+                nc.scalar.activation(out=v[:, t, :], in_=acc[:], func=ACT.Identity, bias=b2t[:, t : t + 1], scale=1.0)
+            h2g = wk.tile([P, 4 * ROWS], BF16, align_bytes=64, tag="h2g")
+            vp = v[:].rearrange("p t c -> p c t")
+            nc.vector.scalar_tensor_tensor(
+                out=h2g[:].rearrange("p (c t) -> p c t", t=4), in0=vp, scalar=SLOPE, in1=vp, op0=ALU.mult, op1=ALU.max
+            )
+            c2 = wk.tile([P, ROWS], U32, align_bytes=64, tag="c2")
+            s2 = wk.tile([P, ROWS], U8, align_bytes=64, tag="s2")
+            nc.vector.quantize_mx(out=c2[:].bitcast(FP8X4), scales=s2[:], in_=h2g[:])
+
+            lg = ps_l.tile([P, J, A], F32, tag="lg")
+            for j in range(J):
+                nc.tensor.matmul_mx(
+                    out=lg[:, j, :],
+                    lhsT=c2[:, P * j : P * (j + 1)].bitcast(FP8X4),
+                    lhsT_scale=s2[:, P * j : P * (j + 1)],
+                    rhs=w3c[:].bitcast(FP8X4),
+                    rhs_scale=w3s[:],
+                    start=True,
+                    stop=True,
+                )
+
+            lm = wk.tile([P, J, A], F32, tag="lm")
+            nc.vector.tensor_tensor(out=lm[:], in0=lg[:], in1=q[:], op=ALU.add)
+            nmx = wk.tile([P, J], F32, tag="nmx")
+            nc.vector.tensor_reduce(out=nmx[:], in_=lm[:], axis=AX.X, op=ALU.max, negate=True)
+            ex = wk.tile([P, J, A], F32, tag="ex")
+            sm = wk.tile([P, J], F32, tag="sm")
+            for j in range(J):
+                nc.scalar.activation(
+                    out=ex[:, j, :], in_=lm[:, j, :], func=ACT.Exp, bias=nmx[:, j : j + 1], scale=1.0,
+                    accum_out=sm[:, j : j + 1],
+                )
+            rs = wk.tile([P, J], F32, tag="rs")
+            nc.vector.reciprocal(out=rs[:], in_=sm[:])
+            ot = wk.tile([P, J, A], F32, tag="ot")
+            for j in range(J):
+                nc.scalar.activation(out=ot[:, j, :], in_=ex[:, j, :], func=ACT.Copy, scale=rs[:, j : j + 1])
+            nc.scalar.dma_start(out=outv[g], in_=ot[:])

@@ -18,28 +18,39 @@ P = 128
 B, A, G, H1, H2 = 8192, 128, 5, 1024, 512
 SLOPE = 0.4
 BIG = 1.0e30
-J = 4
-ROWS = P * J
-NGROUPS = B // ROWS
 FLOPS = 2 * B * (H1 * H2 + H2 * A)
+UNIT_J = [4,4,4,4,4,4,4,4,4,4,4,4,4,4,4,4]
+TEMPLATE = [("Ta",0),("C2",2),("lm",3),("M1",1),("Q2",2),("aa",0),("c1",1),("f",0),("Tb",0),("GS",-1),("mx",3),("M2",2),("Q1a",0),("q",0),("ab",0),("exp",3),("R",4),("Q1b",0),("sc",4),("t",-1)]
+LOAD_LAG = 3
 
 
 def tile_dqn_pa_t_kernel(tc, x, h1, W2, b2, W3, b3, out):
     nc = tc.nc
+    n_units = len(UNIT_J)
+    row0 = [P * sum(UNIT_J[:i]) for i in range(n_units)]
+    assert P * sum(UNIT_J) == B
     with ExitStack() as ctx:
         const = ctx.enter_context(tc.tile_pool(name="const", bufs=1))
         ld = ctx.enter_context(tc.tile_pool(name="ld", bufs=4))
-        wk = ctx.enter_context(tc.tile_pool(name="wk", bufs=2))
-        ps_t = ctx.enter_context(tc.psum_pool(name="ps_t", bufs=2))
-        ps_a = ctx.enter_context(tc.psum_pool(name="ps_a", bufs=4))
-        ps_l = ctx.enter_context(tc.psum_pool(name="ps_l", bufs=1))
+        wk = ctx.enter_context(tc.tile_pool(name="wk", bufs=3))
+        ps = ctx.enter_context(tc.psum_pool(name="ps", bufs=1))
+        ctx.enter_context(tc.manual_schedule())
+        tl = {}
 
-        h1v = h1.rearrange("(g p j) k -> g p j k", p=P, j=J)
-        xv = x.rearrange("(g p j) c -> g p j c", p=P, j=J)
-        outv = out.rearrange("(g p j) a -> g p j a", p=P, j=J)
+        def load(i):
+            J = UNIT_J[i]
+            rows = slice(row0[i], row0[i] + P * J)
+            h1_sb = ld.tile([P, J, H1], BF16, tag="h1")
+            nc.sync.dma_start(out=h1_sb[:], in_=h1[rows, :].rearrange("(p j) k -> p j k", j=J))
+            x_sb = ld.tile([P, J, A * G], BF16, tag="x")
+            nc.sync.dma_start(out=x_sb[:], in_=x[rows, :].rearrange("(p j) c -> p j c", j=J))
+            tl[("h1", i)] = h1_sb
+            tl[("xg", i)] = x_sb[:].rearrange("p j (a e) -> p (j a) e", e=G)
 
         w2raw = const.tile([P, 4, 2 * H2], BF16)
         nc.sync.dma_start(out=w2raw[:], in_=W2.rearrange("(c q e) n -> q c (e n)", c=4, e=2))
+        for i in range(LOAD_LAG):
+            load(i)
         w3raw = const.tile([P, 4, A], BF16)
         nc.scalar.dma_start(out=w3raw[:], in_=W3.rearrange("(p j) a -> p j a", j=4))
         b2bf = const.tile([P, 4], BF16)
@@ -72,96 +83,189 @@ def tile_dqn_pa_t_kernel(tc, x, h1, W2, b2, W3, b3, out):
         nc.vector.tensor_copy(out=b3bc[:], in_=b3bf[:])
         nc.vector.quantize_mx(out=w3c[:].bitcast(FP8X4), scales=w3s[:], in_=w3grp[:].rearrange("p a j -> p (a j)"))
 
-        for g in range(NGROUPS):
-            h1_sb = ld.tile([P, J, H1], BF16, tag="h1")
-            nc.sync.dma_start(out=h1_sb[:], in_=h1v[g])
-            x_sb = ld.tile([P, J, A * G], BF16, tag="x")
-            nc.sync.dma_start(out=x_sb[:], in_=xv[g])
-
-            xg = x_sb[:].rearrange("p j (a e) -> p (j a) e", e=G)
-            t34 = wk.tile([P, ROWS], F32, tag="t34")
-            fz = wk.tile([P, J, A], F32, tag="fz")
-            q = wk.tile([P, J, A], F32, tag="q")
-            nc.gpsimd.tensor_tensor(out=t34[:], in0=xg[:, :, 3], in1=xg[:, :, 4], op=ALU.add)
-            gs = ps_l.tile([P, ROWS], F32, tag="gs")
+        def st_GS(i):
+            J = UNIT_J[i]
+            gs = ps.tile([P, J * A], F32, tag="gs")
             for e in range(3):
-                nc.tensor.matmul(out=gs[:], lhsT=identb[:], rhs=xg[:, :, e], start=(e == 0), stop=(e == 2))
+                nc.tensor.matmul(out=gs[:], lhsT=identb[:], rhs=tl[("xg", i)][:, :, e], start=(e == 0), stop=(e == 2))
+            tl[("gs", i)] = gs
+
+        def st_t(i):
+            J = UNIT_J[i]
+            t4 = wk.tile([P, J * A], F32, tag="t4")
+            nc.vector.tensor_tensor(out=t4[:], in0=tl[("gs", i)][:], in1=tl[("xg", i)][:, :, 3], op=ALU.add)
+            tl[("t4", i)] = t4
+
+        def st_f(i):
+            J = UNIT_J[i]
+            fz = wk.tile([P, J, A], F32, tag="fz", bufs=2)
             nc.vector.scalar_tensor_tensor(
-                out=fz[:].rearrange("p j a -> p (j a)"), in0=gs[:], scalar=-1.0, in1=t34[:],
+                out=fz[:].rearrange("p j a -> p (j a)"), in0=tl[("xg", i)][:, :, 4], scalar=-1.0, in1=tl[("t4", i)][:],
                 op0=ALU.mult, op1=ALU.is_equal,
             )
+            tl[("fz", i)] = fz
+
+        def st_q(i):
+            J = UNIT_J[i]
+            q = wk.tile([P, J, A], F32, tag="q", bufs=5)
             nc.vector.scalar_tensor_tensor(
-                out=q[:], in0=fz[:], scalar=-BIG, in1=b3bc[:].unsqueeze(1).to_broadcast([P, J, A]),
+                out=q[:], in0=tl[("fz", i)][:], scalar=-BIG, in1=b3bc[:].unsqueeze(1).to_broadcast([P, J, A]),
                 op0=ALU.mult, op1=ALU.add,
             )
+            tl[("q", i)] = q
 
-            grp = wk.tile([P, 2, 4 * ROWS], BF16, align_bytes=64, tag="grp")
-            c1 = wk.tile([P, 2, ROWS], U32, align_bytes=64, tag="c1")
-            s1 = wk.tile([P, 2, ROWS], U8, align_bytes=64, tag="s1")
-            for s in range(2):
-                for jp in range(2):
-                    xt = ps_t.tile([P, 2, 2, P], F32, tag="xt")
-                    for jj in range(2):
-                        for u in range(2):
-                            c = 2 * s + u
-                            nc.tensor.transpose(
-                                xt[:, jj, u, :],
-                                h1_sb[:, 2 * jp + jj, :].bitcast(F32)[:, P * c : P * (c + 1)],
-                                ident[:],
-                            )
-                    dst = grp[:, s, :].bitcast(F32).rearrange("p (j r u) -> p j r u", j=J, u=2)
-                    nc.scalar.copy(out=dst[:, 2 * jp : 2 * jp + 2], in_=xt[:].rearrange("p j u r -> p j r u"))
-                nc.vector.quantize_mx(out=c1[:, s, :].bitcast(FP8X4), scales=s1[:, s, :], in_=grp[:, s, :])
+        def transposes(i, s):
+            J = UNIT_J[i]
+            nj = min(J, 2)
+            banks = []
+            for jp in range(J // nj):
+                xt = ps.tile([P, nj, 2, P], F32, tag="xt", bufs=2)
+                for jj in range(nj):
+                    for u in range(2):
+                        c = 2 * s + u
+                        nc.tensor.transpose(
+                            xt[:, jj, u, :],
+                            tl[("h1", i)][:, nj * jp + jj, :].bitcast(F32)[:, P * c : P * (c + 1)],
+                            ident[:],
+                        )
+                banks.append(xt)
+            tl[("xt", i, s)] = banks
 
-            v = wk.tile([P, 4, ROWS], F32, tag="v")
+        def evacuate(i, s):
+            J = UNIT_J[i]
+            nj = min(J, 2)
+            if s == 0:
+                grp = wk.tile([P, 2, 4 * P * J], BF16, align_bytes=64, tag="grp", bufs=2)
+                tl[("grp", i)] = grp
+            dst = tl[("grp", i)][:, s, :].bitcast(F32).rearrange("p (j r u) -> p j r u", j=J, u=2)
+            for jp in range(J // nj):
+                nc.scalar.copy(
+                    out=dst[:, nj * jp : nj * (jp + 1)], in_=tl[("xt", i, s)][jp][:].rearrange("p j u r -> p j r u")
+                )
+
+        def quant1(i, s):
+            J = UNIT_J[i]
+            if s == 0:
+                c1 = wk.tile([P, 2, P * J], U32, align_bytes=64, tag="c1")
+                s1 = wk.tile([P, 2, P * J], U8, align_bytes=64, tag="s1")
+                tl[("c1", i)] = c1
+                tl[("s1", i)] = s1
+            nc.vector.quantize_mx(
+                out=tl[("c1", i)][:, s, :].bitcast(FP8X4), scales=tl[("s1", i)][:, s, :], in_=tl[("grp", i)][:, s, :]
+            )
+
+        def st_M1(i):
+            J = UNIT_J[i]
+            accs = []
             for t in range(4):
-                acc = ps_a.tile([P, ROWS], F32, tag="acc")
+                acc = ps.tile([P, P * J], F32, tag="acc", bufs=4)
                 for s in range(2):
                     nc.tensor.matmul_mx(
                         out=acc[:],
                         lhsT=w2c[:, s, P * t : P * (t + 1)].bitcast(FP8X4),
                         lhsT_scale=w2s[:, s, P * t : P * (t + 1)],
-                        rhs=c1[:, s, :].bitcast(FP8X4),
-                        rhs_scale=s1[:, s, :],
+                        rhs=tl[("c1", i)][:, s, :].bitcast(FP8X4),
+                        rhs_scale=tl[("s1", i)][:, s, :],
                         start=(s == 0),
                         stop=(s == 1),
                     )
-                nc.scalar.activation(out=v[:, t, :], in_=acc[:], func=ACT.Identity, bias=b2t[:, t : t + 1], scale=1.0)
-            h2g = wk.tile([P, 4 * ROWS], BF16, align_bytes=64, tag="h2g")
-            vp = v[:].rearrange("p t c -> p c t")
+                accs.append(acc)
+            tl[("acc", i)] = accs
+
+        def st_c1(i):
+            J = UNIT_J[i]
+            v = wk.tile([P, 4, P * J], F32, tag="v")
+            for t in range(4):
+                nc.scalar.activation(
+                    out=v[:, t, :], in_=tl[("acc", i)][t][:], func=ACT.Identity, bias=b2t[:, t : t + 1], scale=1.0
+                )
+            tl[("v", i)] = v
+
+        def st_C2(i):
+            J = UNIT_J[i]
+            h2g = wk.tile([P, 4 * P * J], BF16, align_bytes=64, tag="h2g", bufs=2)
+            vp = tl[("v", i)][:].rearrange("p t c -> p c t")
             nc.vector.scalar_tensor_tensor(
                 out=h2g[:].rearrange("p (c t) -> p c t", t=4), in0=vp, scalar=SLOPE, in1=vp, op0=ALU.mult, op1=ALU.max
             )
-            c2 = wk.tile([P, ROWS], U32, align_bytes=64, tag="c2")
-            s2 = wk.tile([P, ROWS], U8, align_bytes=64, tag="s2")
-            nc.vector.quantize_mx(out=c2[:].bitcast(FP8X4), scales=s2[:], in_=h2g[:])
+            tl[("h2g", i)] = h2g
 
-            lg = ps_l.tile([P, J, A], F32, tag="lg")
+        def st_Q2(i):
+            J = UNIT_J[i]
+            c2 = wk.tile([P, P * J], U32, align_bytes=64, tag="c2")
+            s2 = wk.tile([P, P * J], U8, align_bytes=64, tag="s2")
+            nc.vector.quantize_mx(out=c2[:].bitcast(FP8X4), scales=s2[:], in_=tl[("h2g", i)][:])
+            tl[("c2", i)] = c2
+            tl[("s2", i)] = s2
+
+        def st_M2(i):
+            J = UNIT_J[i]
+            lg = ps.tile([P, J, A], F32, tag="lg")
             for j in range(J):
                 nc.tensor.matmul_mx(
                     out=lg[:, j, :],
-                    lhsT=c2[:, P * j : P * (j + 1)].bitcast(FP8X4),
-                    lhsT_scale=s2[:, P * j : P * (j + 1)],
+                    lhsT=tl[("c2", i)][:, P * j : P * (j + 1)].bitcast(FP8X4),
+                    lhsT_scale=tl[("s2", i)][:, P * j : P * (j + 1)],
                     rhs=w3c[:].bitcast(FP8X4),
                     rhs_scale=w3s[:],
                     start=True,
                     stop=True,
                 )
+            tl[("lg", i)] = lg
 
+        def st_lm(i):
+            J = UNIT_J[i]
             lm = wk.tile([P, J, A], F32, tag="lm")
-            nc.vector.tensor_tensor(out=lm[:], in0=lg[:], in1=q[:], op=ALU.add)
+            nc.vector.tensor_tensor(out=lm[:], in0=tl[("lg", i)][:], in1=tl[("q", i)][:], op=ALU.add)
+            tl[("lm", i)] = lm
+
+        def st_mx(i):
+            J = UNIT_J[i]
             nmx = wk.tile([P, J], F32, tag="nmx")
-            nc.vector.tensor_reduce(out=nmx[:], in_=lm[:], axis=AX.X, op=ALU.max, negate=True)
+            nc.vector.tensor_reduce(out=nmx[:], in_=tl[("lm", i)][:], axis=AX.X, op=ALU.max, negate=True)
+            tl[("nmx", i)] = nmx
+
+        def st_exp(i):
+            J = UNIT_J[i]
             ex = wk.tile([P, J, A], F32, tag="ex")
             sm = wk.tile([P, J], F32, tag="sm")
             for j in range(J):
                 nc.scalar.activation(
-                    out=ex[:, j, :], in_=lm[:, j, :], func=ACT.Exp, bias=nmx[:, j : j + 1], scale=1.0,
-                    accum_out=sm[:, j : j + 1],
+                    out=ex[:, j, :], in_=tl[("lm", i)][:, j, :], func=ACT.Exp, bias=tl[("nmx", i)][:, j : j + 1],
+                    scale=1.0, accum_out=sm[:, j : j + 1],
                 )
+            tl[("ex", i)] = ex
+            tl[("sm", i)] = sm
+
+        def st_R(i):
+            J = UNIT_J[i]
             rs = wk.tile([P, J], F32, tag="rs")
-            nc.vector.reciprocal(out=rs[:], in_=sm[:])
+            nc.vector.reciprocal(out=rs[:], in_=tl[("sm", i)][:])
+            tl[("rs", i)] = rs
+
+        def st_sc(i):
+            J = UNIT_J[i]
             ot = wk.tile([P, J, A], F32, tag="ot")
             for j in range(J):
-                nc.scalar.activation(out=ot[:, j, :], in_=ex[:, j, :], func=ACT.Copy, scale=rs[:, j : j + 1])
-            nc.scalar.dma_start(out=outv[g], in_=ot[:])
+                nc.scalar.activation(
+                    out=ot[:, j, :], in_=tl[("ex", i)][:, j, :], func=ACT.Copy, scale=tl[("rs", i)][:, j : j + 1]
+                )
+            rows = slice(row0[i], row0[i] + P * J)
+            nc.scalar.dma_start(out=out[rows, :].rearrange("(p j) a -> p j a", j=J), in_=ot[:])
+
+        stages = {
+            "GS": st_GS, "t": st_t, "f": st_f, "q": st_q,
+            "Ta": lambda i: transposes(i, 0), "Tb": lambda i: transposes(i, 1),
+            "aa": lambda i: evacuate(i, 0), "ab": lambda i: evacuate(i, 1),
+            "Q1a": lambda i: quant1(i, 0), "Q1b": lambda i: quant1(i, 1),
+            "M1": st_M1, "c1": st_c1, "C2": st_C2, "Q2": st_Q2, "M2": st_M2,
+            "lm": st_lm, "mx": st_mx, "exp": st_exp, "R": st_R, "sc": st_sc,
+        }
+        lags = [lag for (name, lag) in TEMPLATE]
+        for tick in range(min(lags), n_units + max(lags)):
+            if 0 <= tick and tick + LOAD_LAG < n_units:
+                load(tick + LOAD_LAG)
+            for (name, lag) in TEMPLATE:
+                i = tick - lag
+                if 0 <= i and i < n_units:
+                    stages[name](i)

@@ -246,12 +246,11 @@ def tile_dqn_pa_t_kernel(tc, x, h1, W2, b2, W3, b3, out):
         def st_sc(i):
             J = UNIT_J[i]
             ot = wk.tile([P, J, A], F32, tag="ot")
-            for j in range(J):
-                nc.scalar.activation(
-                    out=ot[:, j, :], in_=tl[("ex", i)][:, j, :], func=ACT.Copy, scale=tl[("rs", i)][:, j : j + 1]
-                )
+            nc.vector.tensor_tensor(
+                out=ot[:], in0=tl[("ex", i)][:], in1=tl[("rs", i)][:].unsqueeze(2).to_broadcast([P, J, A]), op=ALU.mult
+            )
             rows = slice(row0[i], row0[i] + P * J)
-            nc.scalar.dma_start(out=out[rows, :].rearrange("(p j) a -> p j a", j=J), in_=ot[:])
+            nc.sync.dma_start(out=out[rows, :].rearrange("(p j) a -> p j a", j=J), in_=ot[:])
 
         stages = {
             "GS": st_GS, "t": st_t, "f": st_f, "q": st_q,

@@ -137,10 +137,10 @@ def tile_dqn_pa_t_kernel(tc, x, h1, W2, b2, W3, b3, out):
             if s == 0:
                 grp = wk.tile([P, 2, 4 * P * J], BF16, align_bytes=64, tag="grp", bufs=2)
                 tl[("grp", i)] = grp
-            dst = tl[("grp", i)][:, s, :].bitcast(F32).rearrange("p (j r u) -> p j r u", j=J, u=2)
+            dst = tl[("grp", i)][:, s, :].bitcast(F32).rearrange("p (r j u) -> p r j u", j=J, u=2)
             for jp in range(J // nj):
                 nc.scalar.copy(
-                    out=dst[:, nj * jp : nj * (jp + 1)], in_=tl[("xt", i, s)][jp][:].rearrange("p j u r -> p j r u")
+                    out=dst[:, :, nj * jp : nj * (jp + 1), :], in_=tl[("xt", i, s)][jp][:].rearrange("p j u r -> p r j u")
                 )
 
         def quant1(i, s):
@@ -174,19 +174,19 @@ def tile_dqn_pa_t_kernel(tc, x, h1, W2, b2, W3, b3, out):
 
         def st_c1(i):
             J = UNIT_J[i]
-            v = wk.tile([P, 4, P * J], F32, tag="v")
+            v = wk.tile([P, P * J // 4, 4, 4], F32, tag="v")
             for t in range(4):
                 nc.scalar.activation(
-                    out=v[:, t, :], in_=tl[("acc", i)][t][:], func=ACT.Identity, bias=b2t[:, t : t + 1], scale=1.0
+                    out=v[:, :, t, :], in_=tl[("acc", i)][t][:].rearrange("p (cb ci) -> p cb ci", ci=4), func=ACT.Identity, bias=b2t[:, t : t + 1], scale=1.0
                 )
             tl[("v", i)] = v
 
         def st_C2(i):
             J = UNIT_J[i]
-            h2g = wk.tile([P, 4 * P * J], BF16, align_bytes=64, tag="h2g", bufs=2)
-            vp = tl[("v", i)][:].rearrange("p t c -> p c t")
+            h2g = wk.tile([P, 4, P * J], BF16, align_bytes=64, tag="h2g", bufs=2)
+            vp = tl[("v", i)][:].rearrange("p cb t ci -> p (cb t) ci")
             nc.vector.scalar_tensor_tensor(
-                out=h2g[:].rearrange("p (c t) -> p c t", t=4), in0=vp, scalar=SLOPE, in1=vp, op0=ALU.mult, op1=ALU.max
+                out=h2g[:].rearrange("p ci x -> p x ci"), in0=vp, scalar=SLOPE, in1=vp, op0=ALU.mult, op1=ALU.max
             )
             tl[("h2g", i)] = h2g
 
@@ -194,7 +194,7 @@ def tile_dqn_pa_t_kernel(tc, x, h1, W2, b2, W3, b3, out):
             J = UNIT_J[i]
             c2 = wk.tile([P, P * J], U32, align_bytes=64, tag="c2")
             s2 = wk.tile([P, P * J], U8, align_bytes=64, tag="s2")
-            nc.vector.quantize_mx(out=c2[:].bitcast(FP8X4), scales=s2[:], in_=tl[("h2g", i)][:])
+            nc.vector.quantize_mx(out=c2[:].bitcast(FP8X4), scales=s2[:], in_=tl[("h2g", i)][:].rearrange("p ci x -> p (ci x)"))
             tl[("c2", i)] = c2
             tl[("s2", i)] = s2
 
@@ -246,11 +246,12 @@ def tile_dqn_pa_t_kernel(tc, x, h1, W2, b2, W3, b3, out):
         def st_sc(i):
             J = UNIT_J[i]
             ot = wk.tile([P, J, A], F32, tag="ot")
-            nc.vector.tensor_tensor(
-                out=ot[:], in0=tl[("ex", i)][:], in1=tl[("rs", i)][:].unsqueeze(2).to_broadcast([P, J, A]), op=ALU.mult
-            )
+            for j in range(J):
+                nc.scalar.activation(
+                    out=ot[:, j, :], in_=tl[("ex", i)][:, j, :], func=ACT.Copy, scale=tl[("rs", i)][:, j : j + 1]
+                )
             rows = slice(row0[i], row0[i] + P * J)
-            nc.sync.dma_start(out=out[rows, :].rearrange("(p j) a -> p j a", j=J), in_=ot[:])
+            nc.scalar.dma_start(out=out[rows, :].rearrange("(p j) a -> p j a", j=J), in_=ot[:])
 
         stages = {
             "GS": st_GS, "t": st_t, "f": st_f, "q": st_q,

@@ -1,8 +1,6 @@
 from contextlib import ExitStack
 
-import concourse.bass as bass
 import concourse.mybir as mybir
-import concourse.tile as tile
 from concourse.masks import make_identity
 
 F32 = mybir.dt.float32
@@ -15,257 +13,261 @@ ACT = mybir.ActivationFunctionType
 AX = mybir.AxisListType
 
 P = 128
+PACK = 4
 B, A, G, H1, H2 = 8192, 128, 5, 1024, 512
 SLOPE = 0.4
-BIG = 1.0e30
+FORBID = -1.0e30
+PASSES = H1 // (P * PACK)
+TILES = 4
+ROWS = P * TILES
+UNITS = B // ROWS
+AHEAD = 3
+SUMMED_ON_TENSOR = 3
 FLOPS = 2 * B * (H1 * H2 + H2 * A)
-UNIT_J = [4,4,4,4,4,4,4,4,4,4,4,4,4,4,4,4]
-TEMPLATE = [("Ta",0),("C2",2),("lm",3),("M1",1),("Q2",2),("aa",0),("c1",1),("f",0),("Tb",0),("GS",-1),("mx",3),("M2",2),("Q1a",0),("q",0),("ab",0),("exp",3),("R",4),("Q1b",0),("sc",4),("t",-1)]
-LOAD_LAG = 3
 
 
 def tile_dqn_pa_t_kernel(tc, x, h1, W2, b2, W3, b3, out):
     nc = tc.nc
-    n_units = len(UNIT_J)
-    row0 = [P * sum(UNIT_J[:i]) for i in range(n_units)]
-    assert P * sum(UNIT_J) == B
     with ExitStack() as ctx:
         const = ctx.enter_context(tc.tile_pool(name="const", bufs=1))
-        ld = ctx.enter_context(tc.tile_pool(name="ld", bufs=4))
-        wk = ctx.enter_context(tc.tile_pool(name="wk", bufs=3))
-        ps = ctx.enter_context(tc.psum_pool(name="ps", bufs=1))
+        loads = ctx.enter_context(tc.tile_pool(name="loads", bufs=AHEAD + 1))
+        work = ctx.enter_context(tc.tile_pool(name="work", bufs=3))
+        psum = ctx.enter_context(tc.psum_pool(name="psum", bufs=1))
         ctx.enter_context(tc.manual_schedule())
-        tl = {}
+        held = {}
 
-        def load(i):
-            J = UNIT_J[i]
-            rows = slice(row0[i], row0[i] + P * J)
-            h1_sb = ld.tile([P, J, H1], BF16, tag="h1")
-            nc.sync.dma_start(out=h1_sb[:], in_=h1[rows, :].rearrange("(p j) k -> p j k", j=J))
-            x_sb = ld.tile([P, J, A * G], BF16, tag="x")
-            nc.sync.dma_start(out=x_sb[:], in_=x[rows, :].rearrange("(p j) c -> p j c", j=J))
-            tl[("h1", i)] = h1_sb
-            tl[("xg", i)] = x_sb[:].rearrange("p j (a e) -> p (j a) e", e=G)
+        def load(u):
+            rows = slice(ROWS * u, ROWS * (u + 1))
+            h1_sb = loads.tile([P, TILES, H1], BF16, tag="h1")
+            nc.sync.dma_start(out=h1_sb[:], in_=h1[rows, :].rearrange("(j p) k -> p j k", p=P))
+            x_sb = loads.tile([P, TILES, A * G], BF16, tag="x")
+            nc.sync.dma_start(out=x_sb[:], in_=x[rows, :].rearrange("(p j) c -> p j c", j=TILES))
+            held["h1", u] = h1_sb
+            held["x", u] = x_sb[:].rearrange("p j (a e) -> p (j a) e", e=G)
 
-        w2raw = const.tile([P, 4, 2 * H2], BF16)
-        nc.sync.dma_start(out=w2raw[:], in_=W2.rearrange("(c q e) n -> q c (e n)", c=4, e=2))
-        for i in range(LOAD_LAG):
-            load(i)
-        w3raw = const.tile([P, 4, A], BF16)
-        nc.scalar.dma_start(out=w3raw[:], in_=W3.rearrange("(p j) a -> p j a", j=4))
-        b2bf = const.tile([P, 4], BF16)
-        nc.scalar.dma_start(out=b2bf[:], in_=b2.rearrange("(p t) -> p t", t=4))
-        b3bf = const.tile([P, A], BF16)
-        nc.scalar.dma_start(out=b3bf[:], in_=b3.partition_broadcast(P))
+        w2_raw = const.tile([P, PASSES * 2, 2 * H2], BF16)
+        nc.sync.dma_start(out=w2_raw[:], in_=W2.rearrange("(c q e) n -> q c (e n)", c=PASSES * 2, e=2))
+        for u in range(AHEAD):
+            load(u)
+        w3_raw = const.tile([P, PACK, A], BF16)
+        nc.scalar.dma_start(out=w3_raw[:], in_=W3.rearrange("(p t) a -> p t a", t=PACK))
+        b2_bf = const.tile([P, PACK], BF16)
+        nc.scalar.dma_start(out=b2_bf[:], in_=b2.rearrange("(p t) -> p t", t=PACK))
+        b3_bf = const.tile([P, A], BF16)
+        nc.scalar.dma_start(out=b3_bf[:], in_=b3.partition_broadcast(P))
 
-        ident = const.tile([P, P], F32)
-        make_identity(nc, ident[:])
-        identb = const.tile([P, P], BF16)
-        make_identity(nc, identb[:])
+        ident_f32 = const.tile([P, P], F32)
+        make_identity(nc, ident_f32[:])
+        ident_bf = const.tile([P, P], BF16)
+        make_identity(nc, ident_bf[:])
 
-        w2grp = const.tile([P, 2, 4 * H2], BF16, align_bytes=64)
-        w2c = const.tile([P, 2, H2], U32, align_bytes=64)
-        w2s = const.tile([P, 2, H2], U8, align_bytes=64)
-        for s in range(2):
-            nc.vector.tensor_copy(
-                out=w2grp[:, s, :].rearrange("q (t m j) -> q t m j", t=4, j=4),
-                in_=w2raw[:, 2 * s : 2 * s + 2, :].rearrange("q u (e m t) -> q t m (u e)", e=2, t=4),
+        w2_grouped = const.tile([P, PASSES, PACK * H2], BF16, align_bytes=64)
+        w2_words = const.tile([P, PASSES, H2], U32, align_bytes=64)
+        w2_scales = const.tile([P, PASSES, H2], U8, align_bytes=64)
+        for s, copy in ((0, nc.vector.tensor_copy), (1, nc.scalar.copy)):
+            copy(
+                out=w2_grouped[:, s, :].rearrange("q (t m v) -> q t m v", t=PACK, v=PACK),
+                in_=w2_raw[:, 2 * s : 2 * s + 2, :].rearrange("q u (e m t) -> q t m (u e)", e=2, t=PACK),
             )
-        for s in range(2):
-            nc.vector.quantize_mx(out=w2c[:, s, :].bitcast(FP8X4), scales=w2s[:, s, :], in_=w2grp[:, s, :])
-        w3grp = const.tile([P, A, 4], BF16, align_bytes=64)
-        w3c = const.tile([P, A], U32, align_bytes=64)
-        w3s = const.tile([P, A], U8, align_bytes=64)
-        nc.vector.tensor_copy(out=w3grp[:], in_=w3raw[:].rearrange("p j a -> p a j"))
-        b2t = const.tile([P, 4], F32)
-        nc.vector.tensor_copy(out=b2t[:], in_=b2bf[:])
-        b3bc = const.tile([P, A], F32)
-        nc.vector.tensor_copy(out=b3bc[:], in_=b3bf[:])
-        nc.vector.quantize_mx(out=w3c[:].bitcast(FP8X4), scales=w3s[:], in_=w3grp[:].rearrange("p a j -> p (a j)"))
-
-        def st_GS(i):
-            J = UNIT_J[i]
-            gs = ps.tile([P, J * A], F32, tag="gs")
-            for e in range(3):
-                nc.tensor.matmul(out=gs[:], lhsT=identb[:], rhs=tl[("xg", i)][:, :, e], start=(e == 0), stop=(e == 2))
-            tl[("gs", i)] = gs
-
-        def st_t(i):
-            J = UNIT_J[i]
-            t4 = wk.tile([P, J * A], F32, tag="t4")
-            nc.vector.tensor_tensor(out=t4[:], in0=tl[("gs", i)][:], in1=tl[("xg", i)][:, :, 3], op=ALU.add)
-            tl[("t4", i)] = t4
-
-        def st_f(i):
-            J = UNIT_J[i]
-            fz = wk.tile([P, J, A], F32, tag="fz", bufs=2)
-            nc.vector.scalar_tensor_tensor(
-                out=fz[:].rearrange("p j a -> p (j a)"), in0=tl[("xg", i)][:, :, 4], scalar=-1.0, in1=tl[("t4", i)][:],
-                op0=ALU.mult, op1=ALU.is_equal,
-            )
-            tl[("fz", i)] = fz
-
-        def st_q(i):
-            J = UNIT_J[i]
-            q = wk.tile([P, J, A], F32, tag="q", bufs=5)
-            nc.vector.scalar_tensor_tensor(
-                out=q[:], in0=tl[("fz", i)][:], scalar=-BIG, in1=b3bc[:].unsqueeze(1).to_broadcast([P, J, A]),
-                op0=ALU.mult, op1=ALU.add,
-            )
-            tl[("q", i)] = q
-
-        def transposes(i, s):
-            J = UNIT_J[i]
-            nj = min(J, 2)
-            banks = []
-            for jp in range(J // nj):
-                xt = ps.tile([P, nj, 2, P], F32, tag="xt", bufs=2)
-                for jj in range(nj):
-                    for u in range(2):
-                        c = 2 * s + u
-                        nc.tensor.transpose(
-                            xt[:, jj, u, :],
-                            tl[("h1", i)][:, nj * jp + jj, :].bitcast(F32)[:, P * c : P * (c + 1)],
-                            ident[:],
-                        )
-                banks.append(xt)
-            tl[("xt", i, s)] = banks
-
-        def evacuate(i, s):
-            J = UNIT_J[i]
-            nj = min(J, 2)
-            if s == 0:
-                grp = wk.tile([P, 2, 4 * P * J], BF16, align_bytes=64, tag="grp", bufs=2)
-                tl[("grp", i)] = grp
-            dst = tl[("grp", i)][:, s, :].bitcast(F32).rearrange("p (r j u) -> p r j u", j=J, u=2)
-            for jp in range(J // nj):
-                nc.scalar.copy(
-                    out=dst[:, :, nj * jp : nj * (jp + 1), :], in_=tl[("xt", i, s)][jp][:].rearrange("p j u r -> p r j u")
-                )
-
-        def quant1(i, s):
-            J = UNIT_J[i]
-            if s == 0:
-                c1 = wk.tile([P, 2, P * J], U32, align_bytes=64, tag="c1")
-                s1 = wk.tile([P, 2, P * J], U8, align_bytes=64, tag="s1")
-                tl[("c1", i)] = c1
-                tl[("s1", i)] = s1
+        w3_grouped = const.tile([P, A, PACK], BF16, align_bytes=64)
+        w3_words = const.tile([P, A], U32, align_bytes=64)
+        w3_scales = const.tile([P, A], U8, align_bytes=64)
+        nc.vector.tensor_copy(out=w3_grouped[:], in_=w3_raw[:].rearrange("p t a -> p a t"))
+        b2_f32 = const.tile([P, PACK], F32)
+        nc.vector.tensor_copy(out=b2_f32[:], in_=b2_bf[:])
+        b3_f32 = const.tile([P, A], F32)
+        nc.vector.tensor_copy(out=b3_f32[:], in_=b3_bf[:])
+        for s in range(PASSES):
             nc.vector.quantize_mx(
-                out=tl[("c1", i)][:, s, :].bitcast(FP8X4), scales=tl[("s1", i)][:, s, :], in_=tl[("grp", i)][:, s, :]
+                out=w2_words[:, s, :].bitcast(FP8X4), scales=w2_scales[:, s, :], in_=w2_grouped[:, s, :]
             )
+        nc.vector.quantize_mx(
+            out=w3_words[:].bitcast(FP8X4), scales=w3_scales[:], in_=w3_grouped[:].rearrange("p a t -> p (a t)")
+        )
 
-        def st_M1(i):
-            J = UNIT_J[i]
-            accs = []
-            for t in range(4):
-                acc = ps.tile([P, P * J], F32, tag="acc", bufs=4)
-                for s in range(2):
-                    nc.tensor.matmul_mx(
-                        out=acc[:],
-                        lhsT=w2c[:, s, P * t : P * (t + 1)].bitcast(FP8X4),
-                        lhsT_scale=w2s[:, s, P * t : P * (t + 1)],
-                        rhs=tl[("c1", i)][:, s, :].bitcast(FP8X4),
-                        rhs_scale=tl[("s1", i)][:, s, :],
-                        start=(s == 0),
-                        stop=(s == 1),
+        def transpose_h1(u):
+            banks = []
+            for s in range(PASSES):
+                for half in range(TILES // 2):
+                    bank = psum.tile([P, 2, 2, P], F32, tag="bank", bufs=6)
+                    for j in range(2):
+                        for w in range(2):
+                            c = 2 * s + w
+                            nc.tensor.transpose(
+                                bank[:, j, w, :],
+                                held["h1", u][:, 2 * half + j, :].bitcast(F32)[:, P * c : P * (c + 1)],
+                                ident_f32[:],
+                            )
+                    banks.append(bank)
+            held["h1T", u] = banks
+
+        def copy_h1T(u):
+            grouped = work.tile([P, PASSES, PACK * ROWS], BF16, align_bytes=64, tag="grouped", bufs=2)
+            for s in range(PASSES):
+                words = grouped[:, s, :].bitcast(F32).rearrange("p (j r w) -> p j r w", j=TILES, w=2)
+                for half in range(TILES // 2):
+                    nc.scalar.copy(
+                        out=words[:, 2 * half : 2 * half + 2],
+                        in_=held["h1T", u][(TILES // 2) * s + half][:].rearrange("p j w r -> p j r w"),
                     )
-                accs.append(acc)
-            tl[("acc", i)] = accs
+            held["grouped", u] = grouped
 
-        def st_c1(i):
-            J = UNIT_J[i]
-            v = wk.tile([P, P * J // 4, 4, 4], F32, tag="v")
-            for t in range(4):
-                nc.scalar.activation(
-                    out=v[:, :, t, :], in_=tl[("acc", i)][t][:].rearrange("p (cb ci) -> p cb ci", ci=4), func=ACT.Identity, bias=b2t[:, t : t + 1], scale=1.0
+        def quantise_h1(u):
+            h1_words = work.tile([P, PASSES, ROWS], U32, align_bytes=64, tag="h1_words")
+            h1_scales = work.tile([P, PASSES, ROWS], U8, align_bytes=64, tag="h1_scales")
+            for s in range(PASSES):
+                nc.vector.quantize_mx(
+                    out=h1_words[:, s, :].bitcast(FP8X4), scales=h1_scales[:, s, :], in_=held["grouped", u][:, s, :]
                 )
-            tl[("v", i)] = v
+            held["h1_words", u] = h1_words
+            held["h1_scales", u] = h1_scales
 
-        def st_C2(i):
-            J = UNIT_J[i]
-            h2g = wk.tile([P, 4, P * J], BF16, align_bytes=64, tag="h2g", bufs=2)
-            vp = tl[("v", i)][:].rearrange("p cb t ci -> p (cb t) ci")
+        def first_product(u):
+            products = []
+            for t in range(PACK):
+                bank = psum.tile([P, ROWS], F32, tag="bank", bufs=6)
+                for s in range(PASSES):
+                    nc.tensor.matmul_mx(
+                        out=bank[:],
+                        lhsT=w2_words[:, s, P * t : P * (t + 1)].bitcast(FP8X4),
+                        lhsT_scale=w2_scales[:, s, P * t : P * (t + 1)],
+                        rhs=held["h1_words", u][:, s, :].bitcast(FP8X4),
+                        rhs_scale=held["h1_scales", u][:, s, :],
+                        start=(s == 0),
+                        stop=(s == PASSES - 1),
+                    )
+                products.append(bank)
+            held["products", u] = products
+
+        def add_b2(u):
+            v = work.tile([P, ROWS // 4, PACK, 4], F32, tag="v")
+            for t in range(PACK):
+                nc.scalar.activation(
+                    out=v[:, :, t, :],
+                    in_=held["products", u][t][:].rearrange("p (c i) -> p c i", i=4),
+                    func=ACT.Identity,
+                    bias=b2_f32[:, t : t + 1],
+                    scale=1.0,
+                )
+            held["v", u] = v
+
+        def leaky(u):
+            h2 = work.tile([P, TILES, PACK * P], BF16, align_bytes=64, tag="h2", bufs=2)
+            v = held["v", u][:].rearrange("p c t i -> p (c t) i")
             nc.vector.scalar_tensor_tensor(
-                out=h2g[:].rearrange("p ci x -> p x ci"), in0=vp, scalar=SLOPE, in1=vp, op0=ALU.mult, op1=ALU.max
+                out=h2[:].rearrange("p i ct -> p ct i"), in0=v, scalar=SLOPE, in1=v, op0=ALU.mult, op1=ALU.max
             )
-            tl[("h2g", i)] = h2g
+            held["h2", u] = h2
 
-        def st_Q2(i):
-            J = UNIT_J[i]
-            c2 = wk.tile([P, P * J], U32, align_bytes=64, tag="c2")
-            s2 = wk.tile([P, P * J], U8, align_bytes=64, tag="s2")
-            nc.vector.quantize_mx(out=c2[:].bitcast(FP8X4), scales=s2[:], in_=tl[("h2g", i)][:].rearrange("p ci x -> p (ci x)"))
-            tl[("c2", i)] = c2
-            tl[("s2", i)] = s2
+        def quantise_h2(u):
+            h2_words = work.tile([P, ROWS], U32, align_bytes=64, tag="h2_words")
+            h2_scales = work.tile([P, ROWS], U8, align_bytes=64, tag="h2_scales")
+            nc.vector.quantize_mx(
+                out=h2_words[:].bitcast(FP8X4), scales=h2_scales[:], in_=held["h2", u][:].rearrange("p i ct -> p (i ct)")
+            )
+            held["h2_words", u] = h2_words
+            held["h2_scales", u] = h2_scales
 
-        def st_M2(i):
-            J = UNIT_J[i]
-            lg = ps.tile([P, J, A], F32, tag="lg")
-            for j in range(J):
+        def second_product(u):
+            logits = psum.tile([P, TILES, A], F32, tag="logits")
+            for j in range(TILES):
                 nc.tensor.matmul_mx(
-                    out=lg[:, j, :],
-                    lhsT=tl[("c2", i)][:, P * j : P * (j + 1)].bitcast(FP8X4),
-                    lhsT_scale=tl[("s2", i)][:, P * j : P * (j + 1)],
-                    rhs=w3c[:].bitcast(FP8X4),
-                    rhs_scale=w3s[:],
+                    out=logits[:, j, :],
+                    lhsT=held["h2_words", u][:, P * j : P * (j + 1)].bitcast(FP8X4),
+                    lhsT_scale=held["h2_scales", u][:, P * j : P * (j + 1)],
+                    rhs=w3_words[:].bitcast(FP8X4),
+                    rhs_scale=w3_scales[:],
                     start=True,
                     stop=True,
                 )
-            tl[("lg", i)] = lg
+            held["logits", u] = logits
 
-        def st_lm(i):
-            J = UNIT_J[i]
-            lm = wk.tile([P, J, A], F32, tag="lm")
-            nc.vector.tensor_tensor(out=lm[:], in0=tl[("lg", i)][:], in1=tl[("q", i)][:], op=ALU.add)
-            tl[("lm", i)] = lm
-
-        def st_mx(i):
-            J = UNIT_J[i]
-            nmx = wk.tile([P, J], F32, tag="nmx")
-            nc.vector.tensor_reduce(out=nmx[:], in_=tl[("lm", i)][:], axis=AX.X, op=ALU.max, negate=True)
-            tl[("nmx", i)] = nmx
-
-        def st_exp(i):
-            J = UNIT_J[i]
-            ex = wk.tile([P, J, A], F32, tag="ex")
-            sm = wk.tile([P, J], F32, tag="sm")
-            for j in range(J):
-                nc.scalar.activation(
-                    out=ex[:, j, :], in_=tl[("lm", i)][:, j, :], func=ACT.Exp, bias=tl[("nmx", i)][:, j : j + 1],
-                    scale=1.0, accum_out=sm[:, j : j + 1],
+        def sum_on_tensor(u):
+            part = psum.tile([P, ROWS], F32, tag="part")
+            for e in range(SUMMED_ON_TENSOR):
+                nc.tensor.matmul(
+                    out=part[:], lhsT=ident_bf[:], rhs=held["x", u][:, :, e],
+                    start=(e == 0), stop=(e == SUMMED_ON_TENSOR - 1),
                 )
-            tl[("ex", i)] = ex
-            tl[("sm", i)] = sm
+            held["part", u] = part
 
-        def st_R(i):
-            J = UNIT_J[i]
-            rs = wk.tile([P, J], F32, tag="rs")
-            nc.vector.reciprocal(out=rs[:], in_=tl[("sm", i)][:])
-            tl[("rs", i)] = rs
+        def sum_fourth(u):
+            four = work.tile([P, ROWS], F32, tag="four")
+            nc.vector.tensor_tensor(out=four[:], in0=held["part", u][:], in1=held["x", u][:, :, 3], op=ALU.add)
+            held["four", u] = four
 
-        def st_sc(i):
-            J = UNIT_J[i]
-            ot = wk.tile([P, J, A], F32, tag="ot")
-            for j in range(J):
+        def compare(u):
+            zero = work.tile([P, TILES, A], F32, tag="zero", bufs=2)
+            nc.vector.scalar_tensor_tensor(
+                out=zero[:].rearrange("p j a -> p (j a)"), in0=held["x", u][:, :, 4], scalar=-1.0,
+                in1=held["four", u][:], op0=ALU.mult, op1=ALU.is_equal,
+            )
+            held["zero", u] = zero
+
+        def offsets(u):
+            offset = work.tile([P, TILES, A], F32, tag="offset", bufs=5)
+            nc.vector.scalar_tensor_tensor(
+                out=offset[:], in0=held["zero", u][:], scalar=FORBID,
+                in1=b3_f32[:].unsqueeze(1).to_broadcast([P, TILES, A]), op0=ALU.mult, op1=ALU.add,
+            )
+            held["offset", u] = offset
+
+        def masked_logits(u):
+            masked = work.tile([P, TILES, A], F32, tag="masked")
+            nc.vector.tensor_tensor(out=masked[:], in0=held["logits", u][:], in1=held["offset", u][:], op=ALU.add)
+            held["masked", u] = masked
+
+        def row_max(u):
+            minus_max = work.tile([P, TILES], F32, tag="minus_max")
+            nc.vector.tensor_reduce(out=minus_max[:], in_=held["masked", u][:], axis=AX.X, op=ALU.max, negate=True)
+            held["minus_max", u] = minus_max
+
+        def exponentials(u):
+            expo = work.tile([P, TILES, A], F32, tag="expo")
+            total = work.tile([P, TILES], F32, tag="total")
+            for j in range(TILES):
                 nc.scalar.activation(
-                    out=ot[:, j, :], in_=tl[("ex", i)][:, j, :], func=ACT.Copy, scale=tl[("rs", i)][:, j : j + 1]
+                    out=expo[:, j, :], in_=held["masked", u][:, j, :], func=ACT.Exp,
+                    bias=held["minus_max", u][:, j : j + 1], scale=1.0, accum_out=total[:, j : j + 1],
                 )
-            rows = slice(row0[i], row0[i] + P * J)
-            nc.scalar.dma_start(out=out[rows, :].rearrange("(p j) a -> p j a", j=J), in_=ot[:])
+            held["expo", u] = expo
+            held["total", u] = total
 
-        stages = {
-            "GS": st_GS, "t": st_t, "f": st_f, "q": st_q,
-            "Ta": lambda i: transposes(i, 0), "Tb": lambda i: transposes(i, 1),
-            "aa": lambda i: evacuate(i, 0), "ab": lambda i: evacuate(i, 1),
-            "Q1a": lambda i: quant1(i, 0), "Q1b": lambda i: quant1(i, 1),
-            "M1": st_M1, "c1": st_c1, "C2": st_C2, "Q2": st_Q2, "M2": st_M2,
-            "lm": st_lm, "mx": st_mx, "exp": st_exp, "R": st_R, "sc": st_sc,
-        }
-        lags = [lag for (name, lag) in TEMPLATE]
-        for tick in range(min(lags), n_units + max(lags)):
-            if 0 <= tick and tick + LOAD_LAG < n_units:
-                load(tick + LOAD_LAG)
-            for (name, lag) in TEMPLATE:
-                i = tick - lag
-                if 0 <= i and i < n_units:
-                    stages[name](i)
+        def reciprocals(u):
+            inverse = work.tile([P, TILES], F32, tag="inverse")
+            nc.vector.reciprocal(out=inverse[:], in_=held["total", u][:])
+            held["inverse", u] = inverse
+
+        def scale_and_store(u):
+            probs = work.tile([P, TILES, A], F32, tag="probs")
+            for j in range(TILES):
+                nc.scalar.activation(
+                    out=probs[:, j, :], in_=held["expo", u][:, j, :], func=ACT.Copy,
+                    scale=held["inverse", u][:, j : j + 1],
+                )
+            rows = slice(ROWS * u, ROWS * (u + 1))
+            nc.scalar.dma_start(out=out[rows, :].rearrange("(p j) a -> p j a", j=TILES), in_=probs[:])
+
+        def run(stage, u):
+            if 0 <= u < UNITS:
+                stage(u)
+
+        for k in range(-1, UNITS + 4):
+            run(load, k + AHEAD if k >= 0 else UNITS)
+            run(transpose_h1, k)
+            run(copy_h1T, k)
+            run(leaky, k - 2)
+            run(masked_logits, k - 3)
+            run(first_product, k - 1)
+            run(quantise_h2, k - 2)
+            run(add_b2, k - 1)
+            run(compare, k)
+            run(sum_on_tensor, k + 1)
+            run(row_max, k - 3)
+            run(second_product, k - 2)
+            run(quantise_h1, k)
+            run(offsets, k)
+            run(exponentials, k - 3)
+            run(reciprocals, k - 4)
+            run(scale_and_store, k - 4)
+            run(sum_fourth, k + 1)

@@ -22,7 +22,7 @@ TILES = 4
 ROWS = P * TILES
 UNITS = B // ROWS
 AHEAD = 3
-SUMMED_ON_TENSOR = 3
+FOUR_TERM_UNITS = 9
 FLOPS = 2 * B * (H1 * H2 + H2 * A)
 
 
@@ -183,18 +183,19 @@ def tile_dqn_pa_t_kernel(tc, x, h1, W2, b2, W3, b3, out):
             held["logits", u] = logits
 
         def sum_on_tensor(u):
+            terms = 4 if u < FOUR_TERM_UNITS else 3
             part = psum.tile([P, ROWS], F32, tag="part")
-            for e in range(SUMMED_ON_TENSOR):
+            for e in range(terms):
                 nc.tensor.matmul(
-                    out=part[:], lhsT=ident_bf[:], rhs=held["x", u][:, :, e],
-                    start=(e == 0), stop=(e == SUMMED_ON_TENSOR - 1),
+                    out=part[:], lhsT=ident_bf[:], rhs=held["x", u][:, :, e], start=(e == 0), stop=(e == terms - 1)
                 )
-            held["part", u] = part
+            held["four", u] = part
 
         def sum_fourth(u):
-            four = work.tile([P, ROWS], F32, tag="four")
-            nc.vector.tensor_tensor(out=four[:], in0=held["part", u][:], in1=held["x", u][:, :, 3], op=ALU.add)
-            held["four", u] = four
+            if u >= FOUR_TERM_UNITS:
+                four = work.tile([P, ROWS], F32, tag="four")
+                nc.vector.tensor_tensor(out=four[:], in0=held["four", u][:], in1=held["x", u][:, :, 3], op=ALU.add)
+                held["four", u] = four
 
         def compare(u):
             zero = work.tile([P, TILES, A], F32, tag="zero", bufs=2)

@@ -241,13 +241,12 @@ def tile_dqn_pa_t_kernel(tc, x, h1, W2, b2, W3, b3, out):
 
         def scale_and_store(u):
             probs = work.tile([P, TILES, A], F32, tag="probs")
-            for j in range(TILES):
-                nc.scalar.activation(
-                    out=probs[:, j, :], in_=held["expo", u][:, j, :], func=ACT.Copy,
-                    scale=held["inverse", u][:, j : j + 1],
-                )
+            nc.vector.tensor_tensor(
+                out=probs[:], in0=held["expo", u][:], in1=held["inverse", u][:].unsqueeze(2).to_broadcast([P, TILES, A]),
+                op=ALU.mult,
+            )
             rows = slice(ROWS * u, ROWS * (u + 1))
-            nc.scalar.dma_start(out=out[rows, :].rearrange("(p j) a -> p j a", j=TILES), in_=probs[:])
+            nc.sync.dma_start(out=out[rows, :].rearrange("(p j) a -> p j a", j=TILES), in_=probs[:])
 
         def run(stage, u):
             if 0 <= u < UNITS:
@@ -262,6 +261,7 @@ def tile_dqn_pa_t_kernel(tc, x, h1, W2, b2, W3, b3, out):
             run(first_product, k - 1)
             run(quantise_h2, k - 2)
             run(add_b2, k - 1)
+            run(reciprocals, k - 4)
             run(compare, k)
             run(sum_on_tensor, k + 1)
             run(row_max, k - 3)
@@ -269,6 +269,5 @@ def tile_dqn_pa_t_kernel(tc, x, h1, W2, b2, W3, b3, out):
             run(quantise_h1, k)
             run(offsets, k)
             run(exponentials, k - 3)
-            run(reciprocals, k - 4)
             run(scale_and_store, k - 4)
             run(sum_fourth, k + 1)

from contextlib import ExitStack

import concourse.mybir as mybir
from concourse.masks import make_identity

F32 = mybir.dt.float32
BF16 = mybir.dt.bfloat16
U32 = mybir.dt.uint32
U8 = mybir.dt.uint8
FP8X4 = mybir.dt.float8_e4m3fn_x4
ALU = mybir.AluOpType
ACT = mybir.ActivationFunctionType
AX = mybir.AxisListType

P = 128
PACK = 4
B, A, G, H1, H2 = 8192, 128, 5, 1024, 512
SLOPE = 0.4
FORBID = -1.0e30
PASSES = H1 // (P * PACK)
TILES = 4
ROWS = P * TILES
UNITS = B // ROWS
AHEAD = 3
FOUR_TERM_UNITS = 9
FLOPS = 2 * B * (H1 * H2 + H2 * A)


def tile_dqn_pa_t_kernel(tc, x, h1, W2, b2, W3, b3, out):
    nc = tc.nc
    with ExitStack() as ctx:
        const = ctx.enter_context(tc.tile_pool(name="const", bufs=1))
        loads = ctx.enter_context(tc.tile_pool(name="loads", bufs=AHEAD + 1))
        work = ctx.enter_context(tc.tile_pool(name="work", bufs=3))
        psum = ctx.enter_context(tc.psum_pool(name="psum", bufs=1))
        ctx.enter_context(tc.manual_schedule())
        held = {}

        def load(u):
            rows = slice(ROWS * u, ROWS * (u + 1))
            h1_sb = loads.tile([P, TILES, H1], BF16, tag="h1")
            nc.sync.dma_start(out=h1_sb[:], in_=h1[rows, :].rearrange("(j p) k -> p j k", p=P))
            x_sb = loads.tile([P, TILES, A * G], BF16, tag="x")
            nc.sync.dma_start(out=x_sb[:], in_=x[rows, :].rearrange("(p j) c -> p j c", j=TILES))
            held["h1", u] = h1_sb
            held["x", u] = x_sb[:].rearrange("p j (a e) -> p (j a) e", e=G)

        w2_raw = const.tile([P, PASSES * 2, 2 * H2], BF16)
        nc.sync.dma_start(out=w2_raw[:], in_=W2.rearrange("(c q e) n -> q c (e n)", c=PASSES * 2, e=2))
        for u in range(AHEAD):
            load(u)
        w3_raw = const.tile([P, PACK, A], BF16)
        nc.scalar.dma_start(out=w3_raw[:], in_=W3.rearrange("(p t) a -> p t a", t=PACK))
        b2_bf = const.tile([P, PACK], BF16)
        nc.scalar.dma_start(out=b2_bf[:], in_=b2.rearrange("(p t) -> p t", t=PACK))
        b3_bf = const.tile([P, A], BF16)
        nc.scalar.dma_start(out=b3_bf[:], in_=b3.partition_broadcast(P))

        ident_f32 = const.tile([P, P], F32)
        make_identity(nc, ident_f32[:])
        ident_bf = const.tile([P, P], BF16)
        make_identity(nc, ident_bf[:])

        w2_grouped = const.tile([P, PASSES, PACK * H2], BF16, align_bytes=64)
        w2_words = const.tile([P, PASSES, H2], U32, align_bytes=64)
        w2_scales = const.tile([P, PASSES, H2], U8, align_bytes=64)
        for s, copy in ((0, nc.vector.tensor_copy), (1, nc.scalar.copy)):
            copy(
                out=w2_grouped[:, s, :].rearrange("q (t m v) -> q t m v", t=PACK, v=PACK),
                in_=w2_raw[:, 2 * s : 2 * s + 2, :].rearrange("q u (e m t) -> q t m (u e)", e=2, t=PACK),
            )
        w3_grouped = const.tile([P, A, PACK], BF16, align_bytes=64)
        w3_words = const.tile([P, A], U32, align_bytes=64)
        w3_scales = const.tile([P, A], U8, align_bytes=64)
        nc.vector.tensor_copy(out=w3_grouped[:], in_=w3_raw[:].rearrange("p t a -> p a t"))
        b2_f32 = const.tile([P, PACK], F32)
        nc.vector.tensor_copy(out=b2_f32[:], in_=b2_bf[:])
        b3_f32 = const.tile([P, A], F32)
        nc.vector.tensor_copy(out=b3_f32[:], in_=b3_bf[:])
        for s in range(PASSES):
            nc.vector.quantize_mx(
                out=w2_words[:, s, :].bitcast(FP8X4), scales=w2_scales[:, s, :], in_=w2_grouped[:, s, :]
            )
        nc.vector.quantize_mx(
            out=w3_words[:].bitcast(FP8X4), scales=w3_scales[:], in_=w3_grouped[:].rearrange("p a t -> p (a t)")
        )

        def transpose_h1(u):
            banks = []
            for s in range(PASSES):
                for half in range(TILES // 2):
                    bank = psum.tile([P, 2, 2, P], F32, tag="bank", bufs=6)
                    for j in range(2):
                        for w in range(2):
                            c = 2 * s + w
                            nc.tensor.transpose(
                                bank[:, j, w, :],
                                held["h1", u][:, 2 * half + j, :].bitcast(F32)[:, P * c : P * (c + 1)],
                                ident_f32[:],
                            )
                    banks.append(bank)
            held["h1T", u] = banks

        def copy_h1T(u):
            grouped = work.tile([P, PASSES, PACK * ROWS], BF16, align_bytes=64, tag="grouped", bufs=2)
            for s in range(PASSES):
                words = grouped[:, s, :].bitcast(F32).rearrange("p (j r w) -> p j r w", j=TILES, w=2)
                for half in range(TILES // 2):
                    nc.scalar.copy(
                        out=words[:, 2 * half : 2 * half + 2],
                        in_=held["h1T", u][(TILES // 2) * s + half][:].rearrange("p j w r -> p j r w"),
                    )
            held["grouped", u] = grouped

        def quantise_h1(u):
            h1_words = work.tile([P, PASSES, ROWS], U32, align_bytes=64, tag="h1_words")
            h1_scales = work.tile([P, PASSES, ROWS], U8, align_bytes=64, tag="h1_scales")
            for s in range(PASSES):
                nc.vector.quantize_mx(
                    out=h1_words[:, s, :].bitcast(FP8X4), scales=h1_scales[:, s, :], in_=held["grouped", u][:, s, :]
                )
            held["h1_words", u] = h1_words
            held["h1_scales", u] = h1_scales

        def first_product(u):
            products = []
            for t in range(PACK):
                bank = psum.tile([P, ROWS], F32, tag="bank", bufs=6)
                for s in range(PASSES):
                    nc.tensor.matmul_mx(
                        out=bank[:],
                        lhsT=w2_words[:, s, P * t : P * (t + 1)].bitcast(FP8X4),
                        lhsT_scale=w2_scales[:, s, P * t : P * (t + 1)],
                        rhs=held["h1_words", u][:, s, :].bitcast(FP8X4),
                        rhs_scale=held["h1_scales", u][:, s, :],
                        start=(s == 0),
                        stop=(s == PASSES - 1),
                    )
                products.append(bank)
            held["products", u] = products

        def add_b2(u):
            v = work.tile([P, ROWS // 4, PACK, 4], F32, tag="v")
            for t in range(PACK):
                nc.scalar.activation(
                    out=v[:, :, t, :],
                    in_=held["products", u][t][:].rearrange("p (c i) -> p c i", i=4),
                    func=ACT.Identity,
                    bias=b2_f32[:, t : t + 1],
                    scale=1.0,
                )
            held["v", u] = v

        def leaky(u):
            h2 = work.tile([P, TILES, PACK * P], BF16, align_bytes=64, tag="h2", bufs=2)
            v = held["v", u][:].rearrange("p c t i -> p (c t) i")
            nc.vector.scalar_tensor_tensor(
                out=h2[:].rearrange("p i ct -> p ct i"), in0=v, scalar=SLOPE, in1=v, op0=ALU.mult, op1=ALU.max
            )
            held["h2", u] = h2

        def quantise_h2(u):
            h2_words = work.tile([P, ROWS], U32, align_bytes=64, tag="h2_words")
            h2_scales = work.tile([P, ROWS], U8, align_bytes=64, tag="h2_scales")
            nc.vector.quantize_mx(
                out=h2_words[:].bitcast(FP8X4), scales=h2_scales[:], in_=held["h2", u][:].rearrange("p i ct -> p (i ct)")
            )
            held["h2_words", u] = h2_words
            held["h2_scales", u] = h2_scales

        def second_product(u):
            logits = psum.tile([P, TILES, A], F32, tag="logits")
            for j in range(TILES):
                nc.tensor.matmul_mx(
                    out=logits[:, j, :],
                    lhsT=held["h2_words", u][:, P * j : P * (j + 1)].bitcast(FP8X4),
                    lhsT_scale=held["h2_scales", u][:, P * j : P * (j + 1)],
                    rhs=w3_words[:].bitcast(FP8X4),
                    rhs_scale=w3_scales[:],
                    start=True,
                    stop=True,
                )
            held["logits", u] = logits

        def sum_on_tensor(u):
            terms = 4 if u < FOUR_TERM_UNITS else 3
            part = psum.tile([P, ROWS], F32, tag="part")
            for e in range(terms):
                nc.tensor.matmul(
                    out=part[:], lhsT=ident_bf[:], rhs=held["x", u][:, :, e], start=(e == 0), stop=(e == terms - 1)
                )
            held["four", u] = part

        def sum_fourth(u):
            if u >= FOUR_TERM_UNITS:
                four = work.tile([P, ROWS], F32, tag="four")
                nc.vector.tensor_tensor(out=four[:], in0=held["four", u][:], in1=held["x", u][:, :, 3], op=ALU.add)
                held["four", u] = four

        def compare(u):
            zero = work.tile([P, TILES, A], F32, tag="zero", bufs=2)
            nc.vector.scalar_tensor_tensor(
                out=zero[:].rearrange("p j a -> p (j a)"), in0=held["x", u][:, :, 4], scalar=-1.0,
                in1=held["four", u][:], op0=ALU.mult, op1=ALU.is_equal,
            )
            held["zero", u] = zero

        def offsets(u):
            offset = work.tile([P, TILES, A], F32, tag="offset", bufs=5)
            nc.vector.scalar_tensor_tensor(
                out=offset[:], in0=held["zero", u][:], scalar=FORBID,
                in1=b3_f32[:].unsqueeze(1).to_broadcast([P, TILES, A]), op0=ALU.mult, op1=ALU.add,
            )
            held["offset", u] = offset

        def masked_logits(u):
            masked = work.tile([P, TILES, A], F32, tag="masked")
            nc.vector.tensor_tensor(out=masked[:], in0=held["logits", u][:], in1=held["offset", u][:], op=ALU.add)
            held["masked", u] = masked

        def row_max(u):
            minus_max = work.tile([P, TILES], F32, tag="minus_max")
            nc.vector.tensor_reduce(out=minus_max[:], in_=held["masked", u][:], axis=AX.X, op=ALU.max, negate=True)
            held["minus_max", u] = minus_max

        def exponentials(u):
            expo = work.tile([P, TILES, A], F32, tag="expo")
            total = work.tile([P, TILES], F32, tag="total")
            for j in range(TILES):
                nc.scalar.activation(
                    out=expo[:, j, :], in_=held["masked", u][:, j, :], func=ACT.Exp,
                    bias=held["minus_max", u][:, j : j + 1], scale=1.0, accum_out=total[:, j : j + 1],
                )
            held["expo", u] = expo
            held["total", u] = total

        def reciprocals(u):
            inverse = work.tile([P, TILES], F32, tag="inverse")
            nc.vector.reciprocal(out=inverse[:], in_=held["total", u][:])
            held["inverse", u] = inverse

        def scale_and_store(u):
            probs = work.tile([P, TILES, A], F32, tag="probs")
            nc.vector.tensor_tensor(
                out=probs[:], in0=held["expo", u][:], in1=held["inverse", u][:].unsqueeze(2).to_broadcast([P, TILES, A]),
                op=ALU.mult,
            )
            rows = slice(ROWS * u, ROWS * (u + 1))
            nc.sync.dma_start(out=out[rows, :].rearrange("(p j) a -> p j a", j=TILES), in_=probs[:])

        def run(stage, u):
            if 0 <= u < UNITS:
                stage(u)

        for k in range(-1, UNITS + 4):
            run(load, k + AHEAD if k >= 0 else UNITS)
            run(transpose_h1, k)
            run(copy_h1T, k)
            run(leaky, k - 2)
            run(masked_logits, k - 3)
            run(first_product, k - 1)
            run(quantise_h2, k - 2)
            run(add_b2, k - 1)
            run(reciprocals, k - 4)
            run(compare, k)
            run(sum_on_tensor, k + 1)
            run(row_max, k - 3)
            run(second_product, k - 2)
            run(quantise_h1, k)
            run(offsets, k)
            run(exponentials, k - 3)
            run(scale_and_store, k - 4)
            run(sum_fourth, k + 1)
